import numpy as np
import ml_dtypes

BF16 = ml_dtypes.bfloat16


def bf(x):
    return np.asarray(x, np.float32).astype(BF16)


def f32(x):
    return np.asarray(x, np.float32)


def f64(x):
    return np.asarray(x).astype(np.float64)


def striped(idx):
    return np.tile(idx.reshape(-1, 16).T, (8, 1))


C, S, N, P = 256, 256, 128, 256
EPS = 1e-05


def normalize(v, gain, bias):
    mean = v.sum(axis=0, keepdims=True) / P
    std = np.sqrt(((v - mean) ** 2).sum(axis=0, keepdims=True) / (P - 1))
    return gain * ((v - mean) / (std + EPS)) + bias


def setup_inputs():
    return {
        "x": f32(np.random.standard_normal((C, S))),
        "wo": bf(0.25 * np.random.standard_normal((N, P)) / np.sqrt(N)),
        "wp": bf(0.25 * np.random.standard_normal((C, P)) / np.sqrt(C)),
        "gain_o": f32(1.0 + 0.1 * np.random.standard_normal((P, 1))),
        "bias_o": f32(0.1 * np.random.standard_normal((P, 1))),
        "gain_p": f32(1.0 + 0.1 * np.random.standard_normal((P, 1))),
        "bias_p": f32(0.1 * np.random.standard_normal((P, 1))),
        "offs": striped(np.random.permutation(S)[:N]),
    }


def reference(x, wo, wp, gain_o, bias_o, gain_p, bias_p, offs):
    idx = offs[:16].T.reshape(-1)
    xs = f64(x)[:, idx]
    a = (xs @ f64(wo)).sum(axis=0)[:, None]
    d = (xs.T @ f64(wp)).sum(axis=0)[:, None]
    o_sum = normalize(a, f64(gain_o), f64(bias_o)) + 1.0
    p_sum = normalize(d, f64(gain_p), f64(bias_p)) + 1.0
    return o_sum * p_sum.T

@@ -1,0 +1,114 @@
+import concourse.mybir as mybir
+from concourse.masks import make_identity
+
+F32 = mybir.dt.float32
+BF16 = mybir.dt.bfloat16
+U16 = mybir.dt.uint16
+ADD = mybir.AluOpType.add
+SUBTRACT = mybir.AluOpType.subtract
+MULT = mybir.AluOpType.mult
+COPY = mybir.ActivationFunctionType.Copy
+SQRT = mybir.ActivationFunctionType.Sqrt
+
+C, S, N, P = 256, 256, 128, 256
+PART = 128
+C_BLOCKS = C // PART
+P_BLOCKS = P // PART
+EPS = 1e-05
+BN_STATS_DIM = 6
+
+FLOPS = 2 * C * N + 2 * N * P + 2 * C * P + P * P
+
+
+def tile_selfprojection_kernel(tc, x, wo, wp, gain_o, bias_o, gain_p, bias_p, offs, out):
+    nc = tc.nc
+    with tc.tile_pool(name="held", bufs=1) as held, tc.psum_pool(name="psum", bufs=1) as psum:
+        offsets = held.tile([PART, N // 16], U16, name="offsets")
+        nc.sync.dma_start(offsets[:], offs)
+        x_blocks = []
+        for b, queue in enumerate((nc.sync, nc.scalar)):
+            x_block = held.tile([PART, S], F32, name=f"x_block{b}")
+            queue.dma_start(x_block[:], x[b * PART : (b + 1) * PART, :])
+            x_blocks.append(x_block)
+        wo_sb = held.tile([N, P], BF16, name="wo_sb")
+        nc.scalar.dma_start(wo_sb[:], wo)
+        wp_sb = held.tile([PART, C_BLOCKS, P], BF16, name="wp_sb")
+        nc.sync.dma_start(wp_sb[:], wp.rearrange("(b c) q -> c b q", c=PART))
+
+        o_rows = held.tile([2 * P_BLOCKS, PART], F32, name="o_rows")
+        nc.gpsimd.dma_start(o_rows[0:P_BLOCKS, :], gain_o.rearrange("(b p) one -> b (p one)", p=PART))
+        nc.gpsimd.dma_start(o_rows[P_BLOCKS : 2 * P_BLOCKS, :], bias_o.rearrange("(b p) one -> b (p one)", p=PART))
+        gain_p_rep = held.tile([PART, P], F32, name="gain_p_rep")
+        nc.gpsimd.dma_start(gain_p_rep[:], gain_p.rearrange("q one -> (q one)").partition_broadcast(PART))
+        bias_p_rep = held.tile([PART, P], F32, name="bias_p_rep")
+        nc.gpsimd.dma_start(bias_p_rep[:], bias_p.rearrange("q one -> (q one)").partition_broadcast(PART))
+
+        ones = held.tile([PART, PART], F32, name="ones")
+        nc.vector.memset(ones[:], 1.0)
+        identity = held.tile([2 * P_BLOCKS, 2 * P_BLOCKS], F32, name="identity")
+        make_identity(nc, identity[:])
+        o_cols_ps = psum.tile([PART, 2 * P_BLOCKS], F32, name="o_cols_ps")
+        nc.tensor.matmul(o_cols_ps[:], o_rows[:], identity[:], start=True, stop=True)
+        gain_o_col = held.tile([PART, P_BLOCKS], F32, name="gain_o_col")
+        nc.vector.tensor_copy(gain_o_col[:], o_cols_ps[:, 0:P_BLOCKS])
+        shift_o_col = held.tile([PART, P_BLOCKS], F32, name="shift_o_col")
+        nc.vector.tensor_scalar_add(shift_o_col[:], o_cols_ps[:, P_BLOCKS : 2 * P_BLOCKS], 1.0)
+        shift_p_rep = held.tile([PART, P], F32, name="shift_p_rep")
+        nc.gpsimd.tensor_scalar_add(shift_p_rep[:], bias_p_rep[:], 1.0)
+
+        xs = held.tile([PART, C_BLOCKS, N], F32, name="xs")
+        for b in range(C_BLOCKS):
+            nc.scalar.activation(xs[:, b, :], x_blocks[b][:].indirect(offsets[:]), COPY)
+
+        colsum_ps = psum.tile([N, PART], F32, name="colsum_ps")
+        for b in range(C_BLOCKS):
+            nc.tensor.matmul(colsum_ps[:], xs[:, b, :], ones[:], start=(b == 0), stop=(b == C_BLOCKS - 1))
+        colsum_bf = held.tile([N, PART], BF16, name="colsum_bf")
+        nc.scalar.copy(colsum_bf[:], colsum_ps[:])
+
+        rowsum = held.tile([PART, C_BLOCKS], F32, name="rowsum")
+        nc.vector.reduce_sum(rowsum[:], xs[:], axis=mybir.AxisListType.X)
+        rowsum_bf = held.tile([PART, C_BLOCKS, PART], BF16, name="rowsum_bf")
+        nc.vector.tensor_copy(rowsum_bf[:], rowsum[:].unsqueeze(2).to_broadcast([PART, C_BLOCKS, PART]))
+
+        a_rep_ps = psum.tile([PART, P], F32, name="a_rep_ps")
+        nc.tensor.matmul(a_rep_ps[:], colsum_bf[:], wo_sb[:], start=True, stop=True)
+        a_col_ps = psum.tile([PART, P_BLOCKS], F32, name="a_col_ps")
+        for b in range(P_BLOCKS):
+            nc.tensor.matmul(
+                a_col_ps[:, b : b + 1], wo_sb[:, b * PART : (b + 1) * PART], colsum_bf[:, 0:1], start=True, stop=True
+            )
+        d_rep_ps = psum.tile([PART, P], F32, name="d_rep_ps")
+        for b in range(C_BLOCKS):
+            nc.tensor.matmul(
+                d_rep_ps[:], rowsum_bf[:, b, :], wp_sb[:, b, :], start=(b == 0), stop=(b == C_BLOCKS - 1)
+            )
+
+        mean_var = held.tile([PART, 2, 2], F32, name="mean_var")
+        for slot, row_ps in enumerate((a_rep_ps, d_rep_ps)):
+            stats = held.tile([PART, BN_STATS_DIM], F32, name=f"stats{slot}")
+            nc.vector.bn_stats(stats[:], row_ps[:])
+            nc.vector.bn_aggr(mean_var[:, slot, :], stats[:])
+        o_centred = held.tile([PART, P_BLOCKS], F32, name="o_centred")
+        nc.vector.scalar_tensor_tensor(
+            o_centred[:], a_col_ps[:], mean_var[:, 0, 0:1], gain_o_col[:], op0=SUBTRACT, op1=MULT
+        )
+        r_centred = held.tile([PART, P], F32, name="r_centred")
+        nc.vector.scalar_tensor_tensor(
+            r_centred[:], d_rep_ps[:], mean_var[:, 1, 0:1], gain_p_rep[:], op0=SUBTRACT, op1=MULT
+        )
+        inv_std = held.tile([PART, 2], F32, name="inv_std")
+        nc.scalar.activation(inv_std[:], mean_var[:, :, 1], SQRT, scale=P / (P - 1))
+        nc.vector.tensor_scalar_add(inv_std[:], inv_std[:], EPS)
+        nc.vector.reciprocal(inv_std[:], inv_std[:])
+
+        o_col = held.tile([PART, P_BLOCKS], F32, name="o_col")
+        nc.vector.scalar_tensor_tensor(o_col[:], o_centred[:], inv_std[:, 0:1], shift_o_col[:], op0=MULT, op1=ADD)
+        r_rep = held.tile([PART, P], F32, name="r_rep")
+        nc.vector.scalar_tensor_tensor(r_rep[:], r_centred[:], inv_std[:, 1:2], shift_p_rep[:], op0=MULT, op1=ADD)
+        out_block0 = held.tile([PART, P], F32, name="out_block0")
+        nc.vector.tensor_scalar_mul(out_block0[:], r_rep[:], o_col[:, 0:1])
+        nc.sync.dma_start(out[0:PART, :], out_block0[:])
+        out_block1 = held.tile([PART, P], F32, name="out_block1")
+        nc.scalar.activation(out_block1[:], r_rep[:], COPY, scale=o_col[:, 1:2])
+        nc.scalar.dma_start(out[PART : 2 * PART, :], out_block1[:])

@@ -43,6 +43,10 @@ def tile_selfprojection_kernel(tc, x, wo, wp, gain_o, bias_o, gain_p, bias_p, of
         bias_p_rep = held.tile([PART, P], F32, name="bias_p_rep")
         nc.gpsimd.dma_start(bias_p_rep[:], bias_p.rearrange("q one -> (q one)").partition_broadcast(PART))
 
+        scratch = held.tile([PART, 1], F32, name="scratch")
+        nc.vector.memset(scratch[:], 1.0)
+        nc.scalar.activation(scratch[:], scratch[:], SQRT)
+
         ones = held.tile([PART, PART], F32, name="ones")
         nc.vector.memset(ones[:], 1.0)
         identity = held.tile([2 * P_BLOCKS, 2 * P_BLOCKS], F32, name="identity")

@@ -9,6 +9,7 @@ SUBTRACT = mybir.AluOpType.subtract
 MULT = mybir.AluOpType.mult
 COPY = mybir.ActivationFunctionType.Copy
 SQRT = mybir.ActivationFunctionType.Sqrt
+IDENTITY = mybir.ActivationFunctionType.Identity
 
 C, S, N, P = 256, 256, 128, 256
 PART = 128
@@ -36,12 +37,12 @@ def tile_selfprojection_kernel(tc, x, wo, wp, gain_o, bias_o, gain_p, bias_p, of
         nc.sync.dma_start(wp_sb[:], wp.rearrange("(b c) q -> c b q", c=PART))
 
         o_rows = held.tile([2 * P_BLOCKS, PART], F32, name="o_rows")
-        nc.gpsimd.dma_start(o_rows[0:P_BLOCKS, :], gain_o.rearrange("(b p) one -> b (p one)", p=PART))
-        nc.gpsimd.dma_start(o_rows[P_BLOCKS : 2 * P_BLOCKS, :], bias_o.rearrange("(b p) one -> b (p one)", p=PART))
+        nc.scalar.dma_start(o_rows[0:P_BLOCKS, :], gain_o.rearrange("(b p) one -> b (p one)", p=PART))
+        nc.scalar.dma_start(o_rows[P_BLOCKS : 2 * P_BLOCKS, :], bias_o.rearrange("(b p) one -> b (p one)", p=PART))
         gain_p_rep = held.tile([PART, P], F32, name="gain_p_rep")
-        nc.gpsimd.dma_start(gain_p_rep[:], gain_p.rearrange("q one -> (q one)").partition_broadcast(PART))
+        nc.scalar.dma_start(gain_p_rep[:], gain_p.rearrange("q one -> (q one)").partition_broadcast(PART))
         bias_p_rep = held.tile([PART, P], F32, name="bias_p_rep")
-        nc.gpsimd.dma_start(bias_p_rep[:], bias_p.rearrange("q one -> (q one)").partition_broadcast(PART))
+        nc.sync.dma_start(bias_p_rep[:], bias_p.rearrange("q one -> (q one)").partition_broadcast(PART))
 
         scratch = held.tile([PART, 1], F32, name="scratch")
         nc.vector.memset(scratch[:], 1.0)
@@ -57,8 +58,6 @@ def tile_selfprojection_kernel(tc, x, wo, wp, gain_o, bias_o, gain_p, bias_p, of
         nc.vector.tensor_copy(gain_o_col[:], o_cols_ps[:, 0:P_BLOCKS])
         shift_o_col = held.tile([PART, P_BLOCKS], F32, name="shift_o_col")
         nc.vector.tensor_scalar_add(shift_o_col[:], o_cols_ps[:, P_BLOCKS : 2 * P_BLOCKS], 1.0)
-        shift_p_rep = held.tile([PART, P], F32, name="shift_p_rep")
-        nc.gpsimd.tensor_scalar_add(shift_p_rep[:], bias_p_rep[:], 1.0)
 
         xs = held.tile([PART, C_BLOCKS, N], F32, name="xs")
         for b in range(C_BLOCKS):
@@ -108,11 +107,11 @@ def tile_selfprojection_kernel(tc, x, wo, wp, gain_o, bias_o, gain_p, bias_p, of
 
         o_col = held.tile([PART, P_BLOCKS], F32, name="o_col")
         nc.vector.scalar_tensor_tensor(o_col[:], o_centred[:], inv_std[:, 0:1], shift_o_col[:], op0=MULT, op1=ADD)
-        r_rep = held.tile([PART, P], F32, name="r_rep")
-        nc.vector.scalar_tensor_tensor(r_rep[:], r_centred[:], inv_std[:, 1:2], shift_p_rep[:], op0=MULT, op1=ADD)
+        r_less_1 = held.tile([PART, P], F32, name="r_less_1")
+        nc.vector.scalar_tensor_tensor(r_less_1[:], r_centred[:], inv_std[:, 1:2], bias_p_rep[:], op0=MULT, op1=ADD)
         out_block0 = held.tile([PART, P], F32, name="out_block0")
-        nc.vector.tensor_scalar_mul(out_block0[:], r_rep[:], o_col[:, 0:1])
+        nc.vector.tensor_scalar(out_block0[:], r_less_1[:], 1.0, o_col[:, 0:1], op0=ADD, op1=MULT)
         nc.sync.dma_start(out[0:PART, :], out_block0[:])
         out_block1 = held.tile([PART, P], F32, name="out_block1")
-        nc.scalar.activation(out_block1[:], r_rep[:], COPY, scale=o_col[:, 1:2])
+        nc.scalar.activation(out_block1[:], r_less_1[:], IDENTITY, bias=o_col[:, 1:2], scale=o_col[:, 1:2])
         nc.scalar.dma_start(out[PART : 2 * PART, :], out_block1[:])

@@ -31,16 +31,15 @@ def tile_selfprojection_kernel(tc, x, wo, wp, gain_o, bias_o, gain_p, bias_p, of
             x_block = held.tile([PART, S], F32, name=f"x_block{b}")
             queue.dma_start(x_block[:], x[b * PART : (b + 1) * PART, :])
             x_blocks.append(x_block)
-        wo_sb = held.tile([N, P], BF16, name="wo_sb")
-        nc.scalar.dma_start(wo_sb[:], wo)
         wp_sb = held.tile([PART, C_BLOCKS, P], BF16, name="wp_sb")
         nc.sync.dma_start(wp_sb[:], wp.rearrange("(b c) q -> c b q", c=PART))
-
+        wo_sb = held.tile([N, P], BF16, name="wo_sb")
+        nc.sync.dma_start(wo_sb[:], wo)
         o_rows = held.tile([2 * P_BLOCKS, PART], F32, name="o_rows")
-        nc.scalar.dma_start(o_rows[0:P_BLOCKS, :], gain_o.rearrange("(b p) one -> b (p one)", p=PART))
-        nc.scalar.dma_start(o_rows[P_BLOCKS : 2 * P_BLOCKS, :], bias_o.rearrange("(b p) one -> b (p one)", p=PART))
+        nc.sync.dma_start(o_rows[0:P_BLOCKS, :], gain_o.rearrange("(b p) one -> b (p one)", p=PART))
+        nc.sync.dma_start(o_rows[P_BLOCKS : 2 * P_BLOCKS, :], bias_o.rearrange("(b p) one -> b (p one)", p=PART))
         gain_p_rep = held.tile([PART, P], F32, name="gain_p_rep")
-        nc.scalar.dma_start(gain_p_rep[:], gain_p.rearrange("q one -> (q one)").partition_broadcast(PART))
+        nc.sync.dma_start(gain_p_rep[:], gain_p.rearrange("q one -> (q one)").partition_broadcast(PART))
         bias_p_rep = held.tile([PART, P], F32, name="bias_p_rep")
         nc.sync.dma_start(bias_p_rep[:], bias_p.rearrange("q one -> (q one)").partition_broadcast(PART))
 
@@ -48,32 +47,26 @@ def tile_selfprojection_kernel(tc, x, wo, wp, gain_o, bias_o, gain_p, bias_p, of
         nc.vector.memset(scratch[:], 1.0)
         nc.scalar.activation(scratch[:], scratch[:], SQRT)
 
-        ones = held.tile([PART, PART], F32, name="ones")
+        ones = held.tile([PART, 1], F32, name="ones")
         nc.vector.memset(ones[:], 1.0)
         identity = held.tile([2 * P_BLOCKS, 2 * P_BLOCKS], F32, name="identity")
         make_identity(nc, identity[:])
-        o_cols_ps = psum.tile([PART, 2 * P_BLOCKS], F32, name="o_cols_ps")
-        nc.tensor.matmul(o_cols_ps[:], o_rows[:], identity[:], start=True, stop=True)
-        gain_o_col = held.tile([PART, P_BLOCKS], F32, name="gain_o_col")
-        nc.vector.tensor_copy(gain_o_col[:], o_cols_ps[:, 0:P_BLOCKS])
-        shift_o_col = held.tile([PART, P_BLOCKS], F32, name="shift_o_col")
-        nc.vector.tensor_scalar_add(shift_o_col[:], o_cols_ps[:, P_BLOCKS : 2 * P_BLOCKS], 1.0)
 
         xs = held.tile([PART, C_BLOCKS, N], F32, name="xs")
-        for b in range(C_BLOCKS):
-            nc.scalar.activation(xs[:, b, :], x_blocks[b][:].indirect(offsets[:]), COPY)
-
-        colsum_ps = psum.tile([N, PART], F32, name="colsum_ps")
-        for b in range(C_BLOCKS):
-            nc.tensor.matmul(colsum_ps[:], xs[:, b, :], ones[:], start=(b == 0), stop=(b == C_BLOCKS - 1))
-        colsum_bf = held.tile([N, PART], BF16, name="colsum_bf")
-        nc.scalar.copy(colsum_bf[:], colsum_ps[:])
-
+        colsum_ps = psum.tile([N, 1], F32, name="colsum_ps")
         rowsum = held.tile([PART, C_BLOCKS], F32, name="rowsum")
-        nc.vector.reduce_sum(rowsum[:], xs[:], axis=mybir.AxisListType.X)
         rowsum_bf = held.tile([PART, C_BLOCKS, PART], BF16, name="rowsum_bf")
-        nc.vector.tensor_copy(rowsum_bf[:], rowsum[:].unsqueeze(2).to_broadcast([PART, C_BLOCKS, PART]))
+        d_rep_ps = psum.tile([PART, P], F32, name="d_rep_ps")
+        for b in range(C_BLOCKS):
+            first, last = b == 0, b == C_BLOCKS - 1
+            nc.scalar.activation(xs[:, b, :], x_blocks[b][:].indirect(offsets[:]), COPY)
+            nc.tensor.matmul(colsum_ps[:], xs[:, b, :], ones[:], start=first, stop=last)
+            nc.vector.reduce_sum(rowsum[:, b : b + 1], xs[:, b, :], axis=mybir.AxisListType.X)
+            nc.vector.tensor_copy(rowsum_bf[:, b, :], rowsum[:, b : b + 1].to_broadcast([PART, PART]))
+            nc.tensor.matmul(d_rep_ps[:], rowsum_bf[:, b, :], wp_sb[:, b, :], start=first, stop=last)
 
+        colsum_bf = held.tile([N, PART], BF16, name="colsum_bf")
+        nc.scalar.copy(colsum_bf[:], colsum_ps[:].to_broadcast([N, PART]))
         a_rep_ps = psum.tile([PART, P], F32, name="a_rep_ps")
         nc.tensor.matmul(a_rep_ps[:], colsum_bf[:], wo_sb[:], start=True, stop=True)
         a_col_ps = psum.tile([PART, P_BLOCKS], F32, name="a_col_ps")
@@ -81,34 +74,36 @@ def tile_selfprojection_kernel(tc, x, wo, wp, gain_o, bias_o, gain_p, bias_p, of
             nc.tensor.matmul(
                 a_col_ps[:, b : b + 1], wo_sb[:, b * PART : (b + 1) * PART], colsum_bf[:, 0:1], start=True, stop=True
             )
-        d_rep_ps = psum.tile([PART, P], F32, name="d_rep_ps")
-        for b in range(C_BLOCKS):
-            nc.tensor.matmul(
-                d_rep_ps[:], rowsum_bf[:, b, :], wp_sb[:, b, :], start=(b == 0), stop=(b == C_BLOCKS - 1)
-            )
+
+        o_cols_ps = psum.tile([PART, 2 * P_BLOCKS], F32, name="o_cols_ps")
+        nc.tensor.matmul(o_cols_ps[:], o_rows[:], identity[:], start=True, stop=True)
+        gain_o_col = held.tile([PART, P_BLOCKS], F32, name="gain_o_col")
+        nc.vector.tensor_copy(gain_o_col[:], o_cols_ps[:, 0:P_BLOCKS])
+        shift_o_col = held.tile([PART, P_BLOCKS], F32, name="shift_o_col")
+        nc.vector.tensor_scalar_add(shift_o_col[:], o_cols_ps[:, P_BLOCKS : 2 * P_BLOCKS], 1.0)
 
         mean_var = held.tile([PART, 2, 2], F32, name="mean_var")
-        for slot, row_ps in enumerate((a_rep_ps, d_rep_ps)):
+        for slot, row_ps in enumerate((d_rep_ps, a_rep_ps)):
             stats = held.tile([PART, BN_STATS_DIM], F32, name=f"stats{slot}")
             nc.vector.bn_stats(stats[:], row_ps[:])
             nc.vector.bn_aggr(mean_var[:, slot, :], stats[:])
-        o_centred = held.tile([PART, P_BLOCKS], F32, name="o_centred")
-        nc.vector.scalar_tensor_tensor(
-            o_centred[:], a_col_ps[:], mean_var[:, 0, 0:1], gain_o_col[:], op0=SUBTRACT, op1=MULT
-        )
-        r_centred = held.tile([PART, P], F32, name="r_centred")
-        nc.vector.scalar_tensor_tensor(
-            r_centred[:], d_rep_ps[:], mean_var[:, 1, 0:1], gain_p_rep[:], op0=SUBTRACT, op1=MULT
-        )
         inv_std = held.tile([PART, 2], F32, name="inv_std")
         nc.scalar.activation(inv_std[:], mean_var[:, :, 1], SQRT, scale=P / (P - 1))
+        r_centred = held.tile([PART, P], F32, name="r_centred")
+        nc.vector.scalar_tensor_tensor(
+            r_centred[:], d_rep_ps[:], mean_var[:, 0, 0:1], gain_p_rep[:], op0=SUBTRACT, op1=MULT
+        )
+        o_centred = held.tile([PART, P_BLOCKS], F32, name="o_centred")
+        nc.vector.scalar_tensor_tensor(
+            o_centred[:], a_col_ps[:], mean_var[:, 1, 0:1], gain_o_col[:], op0=SUBTRACT, op1=MULT
+        )
         nc.vector.tensor_scalar_add(inv_std[:], inv_std[:], EPS)
         nc.vector.reciprocal(inv_std[:], inv_std[:])
 
         o_col = held.tile([PART, P_BLOCKS], F32, name="o_col")
-        nc.vector.scalar_tensor_tensor(o_col[:], o_centred[:], inv_std[:, 0:1], shift_o_col[:], op0=MULT, op1=ADD)
+        nc.vector.scalar_tensor_tensor(o_col[:], o_centred[:], inv_std[:, 1:2], shift_o_col[:], op0=MULT, op1=ADD)
         r_less_1 = held.tile([PART, P], F32, name="r_less_1")
-        nc.vector.scalar_tensor_tensor(r_less_1[:], r_centred[:], inv_std[:, 1:2], bias_p_rep[:], op0=MULT, op1=ADD)
+        nc.vector.scalar_tensor_tensor(r_less_1[:], r_centred[:], inv_std[:, 0:1], bias_p_rep[:], op0=MULT, op1=ADD)
         out_block0 = held.tile([PART, P], F32, name="out_block0")
         nc.vector.tensor_scalar(out_block0[:], r_less_1[:], 1.0, o_col[:, 0:1], op0=ADD, op1=MULT)
         nc.sync.dma_start(out[0:PART, :], out_block0[:])

@@ -16,7 +16,8 @@ PART = 128
 C_BLOCKS = C // PART
 P_BLOCKS = P // PART
 EPS = 1e-05
-BN_STATS_DIM = 6
+D, A = 0, 1
+MEAN, SQ_DEV = 1, 2
 
 FLOPS = 2 * C * N + 2 * N * P + 2 * C * P + P * P
 
@@ -56,19 +57,18 @@ def tile_selfprojection_kernel(tc, x, wo, wp, gain_o, bias_o, gain_p, bias_p, of
         colsum_ps = psum.tile([N, 1], F32, name="colsum_ps")
         rowsum = held.tile([PART, C_BLOCKS], F32, name="rowsum")
         rowsum_bf = held.tile([PART, C_BLOCKS, PART], BF16, name="rowsum_bf")
-        d_rep_ps = psum.tile([PART, P], F32, name="d_rep_ps")
+        rows_ps = psum.tile([PART, 2, P], F32, name="rows_ps")
         for b in range(C_BLOCKS):
             first, last = b == 0, b == C_BLOCKS - 1
             nc.scalar.activation(xs[:, b, :], x_blocks[b][:].indirect(offsets[:]), COPY)
             nc.tensor.matmul(colsum_ps[:], xs[:, b, :], ones[:], start=first, stop=last)
             nc.vector.reduce_sum(rowsum[:, b : b + 1], xs[:, b, :], axis=mybir.AxisListType.X)
             nc.vector.tensor_copy(rowsum_bf[:, b, :], rowsum[:, b : b + 1].to_broadcast([PART, PART]))
-            nc.tensor.matmul(d_rep_ps[:], rowsum_bf[:, b, :], wp_sb[:, b, :], start=first, stop=last)
+            nc.tensor.matmul(rows_ps[:, D, :], rowsum_bf[:, b, :], wp_sb[:, b, :], start=first, stop=last)
 
         colsum_bf = held.tile([N, PART], BF16, name="colsum_bf")
         nc.scalar.copy(colsum_bf[:], colsum_ps[:].to_broadcast([N, PART]))
-        a_rep_ps = psum.tile([PART, P], F32, name="a_rep_ps")
-        nc.tensor.matmul(a_rep_ps[:], colsum_bf[:], wo_sb[:], start=True, stop=True)
+        nc.tensor.matmul(rows_ps[:, A, :], colsum_bf[:], wo_sb[:], start=True, stop=True)
         a_col_ps = psum.tile([PART, P_BLOCKS], F32, name="a_col_ps")
         for b in range(P_BLOCKS):
             nc.tensor.matmul(
@@ -82,28 +82,26 @@ def tile_selfprojection_kernel(tc, x, wo, wp, gain_o, bias_o, gain_p, bias_p, of
         shift_o_col = held.tile([PART, P_BLOCKS], F32, name="shift_o_col")
         nc.vector.tensor_scalar_add(shift_o_col[:], o_cols_ps[:, P_BLOCKS : 2 * P_BLOCKS], 1.0)
 
-        mean_var = held.tile([PART, 2, 2], F32, name="mean_var")
-        for slot, row_ps in enumerate((d_rep_ps, a_rep_ps)):
-            stats = held.tile([PART, BN_STATS_DIM], F32, name=f"stats{slot}")
-            nc.vector.bn_stats(stats[:], row_ps[:])
-            nc.vector.bn_aggr(mean_var[:, slot, :], stats[:])
+        stats_flat = held.tile([PART, 2 * 3], F32, name="stats_flat")
+        nc.vector.bn_stats(stats_flat[:], rows_ps[:].rearrange("m slot q -> m q slot"))
+        stats = stats_flat[:].rearrange("m (slot k) -> m slot k", slot=2)
         inv_std = held.tile([PART, 2], F32, name="inv_std")
-        nc.scalar.activation(inv_std[:], mean_var[:, :, 1], SQRT, scale=P / (P - 1))
+        nc.scalar.activation(inv_std[:], stats[:, :, SQ_DEV], SQRT, scale=1.0 / (P - 1))
         r_centred = held.tile([PART, P], F32, name="r_centred")
         nc.vector.scalar_tensor_tensor(
-            r_centred[:], d_rep_ps[:], mean_var[:, 0, 0:1], gain_p_rep[:], op0=SUBTRACT, op1=MULT
+            r_centred[:], rows_ps[:, D, :], stats[:, D, MEAN : MEAN + 1], gain_p_rep[:], op0=SUBTRACT, op1=MULT
         )
         o_centred = held.tile([PART, P_BLOCKS], F32, name="o_centred")
         nc.vector.scalar_tensor_tensor(
-            o_centred[:], a_col_ps[:], mean_var[:, 1, 0:1], gain_o_col[:], op0=SUBTRACT, op1=MULT
+            o_centred[:], a_col_ps[:], stats[:, A, MEAN : MEAN + 1], gain_o_col[:], op0=SUBTRACT, op1=MULT
         )
         nc.vector.tensor_scalar_add(inv_std[:], inv_std[:], EPS)
         nc.vector.reciprocal(inv_std[:], inv_std[:])
 
         o_col = held.tile([PART, P_BLOCKS], F32, name="o_col")
-        nc.vector.scalar_tensor_tensor(o_col[:], o_centred[:], inv_std[:, 1:2], shift_o_col[:], op0=MULT, op1=ADD)
+        nc.vector.scalar_tensor_tensor(o_col[:], o_centred[:], inv_std[:, A : A + 1], shift_o_col[:], op0=MULT, op1=ADD)
         r_less_1 = held.tile([PART, P], F32, name="r_less_1")
-        nc.vector.scalar_tensor_tensor(r_less_1[:], r_centred[:], inv_std[:, 0:1], bias_p_rep[:], op0=MULT, op1=ADD)
+        nc.vector.scalar_tensor_tensor(r_less_1[:], r_centred[:], inv_std[:, D : D + 1], bias_p_rep[:], op0=MULT, op1=ADD)
         out_block0 = held.tile([PART, P], F32, name="out_block0")
         nc.vector.tensor_scalar(out_block0[:], r_less_1[:], 1.0, o_col[:, 0:1], op0=ADD, op1=MULT)
         nc.sync.dma_start(out[0:PART, :], out_block0[:])

@@ -16,8 +16,7 @@ PART = 128
 C_BLOCKS = C // PART
 P_BLOCKS = P // PART
 EPS = 1e-05
-D, A = 0, 1
-MEAN, SQ_DEV = 1, 2
+BN_STATS_DIM = 6
 
 FLOPS = 2 * C * N + 2 * N * P + 2 * C * P + P * P
 
@@ -25,13 +24,13 @@ FLOPS = 2 * C * N + 2 * N * P + 2 * C * P + P * P
 def tile_selfprojection_kernel(tc, x, wo, wp, gain_o, bias_o, gain_p, bias_p, offs, out):
     nc = tc.nc
     with tc.tile_pool(name="held", bufs=1) as held, tc.psum_pool(name="psum", bufs=1) as psum:
-        offsets = held.tile([PART, N // 16], U16, name="offsets")
-        nc.sync.dma_start(offsets[:], offs)
         x_blocks = []
         for b, queue in enumerate((nc.sync, nc.scalar)):
             x_block = held.tile([PART, S], F32, name=f"x_block{b}")
             queue.dma_start(x_block[:], x[b * PART : (b + 1) * PART, :])
             x_blocks.append(x_block)
+        offsets = held.tile([PART, N // 16], U16, name="offsets")
+        nc.sync.dma_start(offsets[:], offs)
         wp_sb = held.tile([PART, C_BLOCKS, P], BF16, name="wp_sb")
         nc.sync.dma_start(wp_sb[:], wp.rearrange("(b c) q -> c b q", c=PART))
         wo_sb = held.tile([N, P], BF16, name="wo_sb")
@@ -57,18 +56,19 @@ def tile_selfprojection_kernel(tc, x, wo, wp, gain_o, bias_o, gain_p, bias_p, of
         colsum_ps = psum.tile([N, 1], F32, name="colsum_ps")
         rowsum = held.tile([PART, C_BLOCKS], F32, name="rowsum")
         rowsum_bf = held.tile([PART, C_BLOCKS, PART], BF16, name="rowsum_bf")
-        rows_ps = psum.tile([PART, 2, P], F32, name="rows_ps")
+        d_rep_ps = psum.tile([PART, P], F32, name="d_rep_ps")
         for b in range(C_BLOCKS):
             first, last = b == 0, b == C_BLOCKS - 1
             nc.scalar.activation(xs[:, b, :], x_blocks[b][:].indirect(offsets[:]), COPY)
             nc.tensor.matmul(colsum_ps[:], xs[:, b, :], ones[:], start=first, stop=last)
             nc.vector.reduce_sum(rowsum[:, b : b + 1], xs[:, b, :], axis=mybir.AxisListType.X)
             nc.vector.tensor_copy(rowsum_bf[:, b, :], rowsum[:, b : b + 1].to_broadcast([PART, PART]))
-            nc.tensor.matmul(rows_ps[:, D, :], rowsum_bf[:, b, :], wp_sb[:, b, :], start=first, stop=last)
+            nc.tensor.matmul(d_rep_ps[:], rowsum_bf[:, b, :], wp_sb[:, b, :], start=first, stop=last)
 
         colsum_bf = held.tile([N, PART], BF16, name="colsum_bf")
         nc.scalar.copy(colsum_bf[:], colsum_ps[:].to_broadcast([N, PART]))
-        nc.tensor.matmul(rows_ps[:, A, :], colsum_bf[:], wo_sb[:], start=True, stop=True)
+        a_rep_ps = psum.tile([PART, P], F32, name="a_rep_ps")
+        nc.tensor.matmul(a_rep_ps[:], colsum_bf[:], wo_sb[:], start=True, stop=True)
         a_col_ps = psum.tile([PART, P_BLOCKS], F32, name="a_col_ps")
         for b in range(P_BLOCKS):
             nc.tensor.matmul(
@@ -82,26 +82,31 @@ def tile_selfprojection_kernel(tc, x, wo, wp, gain_o, bias_o, gain_p, bias_p, of
         shift_o_col = held.tile([PART, P_BLOCKS], F32, name="shift_o_col")
         nc.vector.tensor_scalar_add(shift_o_col[:], o_cols_ps[:, P_BLOCKS : 2 * P_BLOCKS], 1.0)
 
-        stats_flat = held.tile([PART, 2 * 3], F32, name="stats_flat")
-        nc.vector.bn_stats(stats_flat[:], rows_ps[:].rearrange("m slot q -> m q slot"))
-        stats = stats_flat[:].rearrange("m (slot k) -> m slot k", slot=2)
+        mean_var = held.tile([PART, 2, 2], F32, name="mean_var")
+        for slot, row_ps in enumerate((d_rep_ps, a_rep_ps)):
+            stats = held.tile([PART, BN_STATS_DIM], F32, name=f"stats{slot}")
+            nc.vector.bn_stats(stats[:], row_ps[:])
+            nc.vector.bn_aggr(mean_var[:, slot, :], stats[:])
         inv_std = held.tile([PART, 2], F32, name="inv_std")
-        nc.scalar.activation(inv_std[:], stats[:, :, SQ_DEV], SQRT, scale=1.0 / (P - 1))
+        nc.scalar.activation(inv_std[:], mean_var[:, :, 1], SQRT, scale=P / (P - 1))
         r_centred = held.tile([PART, P], F32, name="r_centred")
         nc.vector.scalar_tensor_tensor(
-            r_centred[:], rows_ps[:, D, :], stats[:, D, MEAN : MEAN + 1], gain_p_rep[:], op0=SUBTRACT, op1=MULT
+            r_centred[:], d_rep_ps[:], mean_var[:, 0, 0:1], gain_p_rep[:], op0=SUBTRACT, op1=MULT
         )
         o_centred = held.tile([PART, P_BLOCKS], F32, name="o_centred")
         nc.vector.scalar_tensor_tensor(
-            o_centred[:], a_col_ps[:], stats[:, A, MEAN : MEAN + 1], gain_o_col[:], op0=SUBTRACT, op1=MULT
+            o_centred[:], a_col_ps[:], mean_var[:, 1, 0:1], gain_o_col[:], op0=SUBTRACT, op1=MULT
         )
         nc.vector.tensor_scalar_add(inv_std[:], inv_std[:], EPS)
         nc.vector.reciprocal(inv_std[:], inv_std[:])
 
         o_col = held.tile([PART, P_BLOCKS], F32, name="o_col")
-        nc.vector.scalar_tensor_tensor(o_col[:], o_centred[:], inv_std[:, A : A + 1], shift_o_col[:], op0=MULT, op1=ADD)
+        for b in range(P_BLOCKS):
+            nc.scalar.activation(
+                o_col[:, b : b + 1], o_centred[:, b : b + 1], IDENTITY, bias=shift_o_col[:, b : b + 1], scale=inv_std[:, 1:2]
+            )
         r_less_1 = held.tile([PART, P], F32, name="r_less_1")
-        nc.vector.scalar_tensor_tensor(r_less_1[:], r_centred[:], inv_std[:, D : D + 1], bias_p_rep[:], op0=MULT, op1=ADD)
+        nc.vector.scalar_tensor_tensor(r_less_1[:], r_centred[:], inv_std[:, 0:1], bias_p_rep[:], op0=MULT, op1=ADD)
         out_block0 = held.tile([PART, P], F32, name="out_block0")
         nc.vector.tensor_scalar(out_block0[:], r_less_1[:], 1.0, o_col[:, 0:1], op0=ADD, op1=MULT)
         nc.sync.dma_start(out[0:PART, :], out_block0[:])

@@ -16,6 +16,8 @@ PART = 128
 C_BLOCKS = C // PART
 P_BLOCKS = P // PART
 EPS = 1e-05
+MAX_MOVING = 512
+WARM_UP_MATMULS = 5
 BN_STATS_DIM = 6
 
 FLOPS = 2 * C * N + 2 * N * P + 2 * C * P + P * P
@@ -46,6 +48,12 @@ def tile_selfprojection_kernel(tc, x, wo, wp, gain_o, bias_o, gain_p, bias_p, of
         scratch = held.tile([PART, 1], F32, name="scratch")
         nc.vector.memset(scratch[:], 1.0)
         nc.scalar.activation(scratch[:], scratch[:], SQRT)
+
+        zeros = held.tile([PART, MAX_MOVING], BF16, name="zeros")
+        nc.vector.memset(zeros[:], 0.0)
+        unread_ps = psum.tile([PART, MAX_MOVING], F32, name="unread_ps")
+        for w in range(WARM_UP_MATMULS):
+            nc.tensor.matmul(unread_ps[:], zeros[:, 0:PART], zeros[:], start=True, stop=True)
 
         ones = held.tile([PART, 1], F32, name="ones")
         nc.vector.memset(ones[:], 1.0)

@@ -16,8 +16,7 @@ PART = 128
 C_BLOCKS = C // PART
 P_BLOCKS = P // PART
 EPS = 1e-05
-MAX_MOVING = 512
-WARM_UP_MATMULS = 5
+WARM_UP_MATMULS = 20
 BN_STATS_DIM = 6
 
 FLOPS = 2 * C * N + 2 * N * P + 2 * C * P + P * P
@@ -45,15 +44,15 @@ def tile_selfprojection_kernel(tc, x, wo, wp, gain_o, bias_o, gain_p, bias_p, of
         bias_p_rep = held.tile([PART, P], F32, name="bias_p_rep")
         nc.sync.dma_start(bias_p_rep[:], bias_p.rearrange("q one -> (q one)").partition_broadcast(PART))
 
+        zeros = held.tile([PART, PART], BF16, name="zeros")
+        nc.vector.memset(zeros[:], 0.0)
+        unread_ps = psum.tile([PART, PART], F32, name="unread_ps")
+        for w in range(WARM_UP_MATMULS):
+            nc.tensor.matmul(unread_ps[:], zeros[:], zeros[:], start=True, stop=True)
+
         scratch = held.tile([PART, 1], F32, name="scratch")
         nc.vector.memset(scratch[:], 1.0)
         nc.scalar.activation(scratch[:], scratch[:], SQRT)
-
-        zeros = held.tile([PART, MAX_MOVING], BF16, name="zeros")
-        nc.vector.memset(zeros[:], 0.0)
-        unread_ps = psum.tile([PART, MAX_MOVING], F32, name="unread_ps")
-        for w in range(WARM_UP_MATMULS):
-            nc.tensor.matmul(unread_ps[:], zeros[:, 0:PART], zeros[:], start=True, stop=True)
 
         ones = held.tile([PART, 1], F32, name="ones")
         nc.vector.memset(ones[:], 1.0)

@@ -1,5 +1,4 @@
 import concourse.mybir as mybir
-from concourse.masks import make_identity
 
 F32 = mybir.dt.float32
 BF16 = mybir.dt.bfloat16
@@ -36,9 +35,10 @@ def tile_selfprojection_kernel(tc, x, wo, wp, gain_o, bias_o, gain_p, bias_p, of
         nc.sync.dma_start(wp_sb[:], wp.rearrange("(b c) q -> c b q", c=PART))
         wo_sb = held.tile([N, P], BF16, name="wo_sb")
         nc.sync.dma_start(wo_sb[:], wo)
-        o_rows = held.tile([2 * P_BLOCKS, PART], F32, name="o_rows")
-        nc.sync.dma_start(o_rows[0:P_BLOCKS, :], gain_o.rearrange("(b p) one -> b (p one)", p=PART))
-        nc.sync.dma_start(o_rows[P_BLOCKS : 2 * P_BLOCKS, :], bias_o.rearrange("(b p) one -> b (p one)", p=PART))
+        gain_o_col = held.tile([PART, P_BLOCKS], F32, name="gain_o_col")
+        nc.sync.dma_start(gain_o_col[:], gain_o.rearrange("(b p) one -> p (b one)", p=PART))
+        bias_o_col = held.tile([PART, P_BLOCKS], F32, name="bias_o_col")
+        nc.sync.dma_start(bias_o_col[:], bias_o.rearrange("(b p) one -> p (b one)", p=PART))
         gain_p_rep = held.tile([PART, P], F32, name="gain_p_rep")
         nc.sync.dma_start(gain_p_rep[:], gain_p.rearrange("q one -> (q one)").partition_broadcast(PART))
         bias_p_rep = held.tile([PART, P], F32, name="bias_p_rep")
@@ -56,38 +56,32 @@ def tile_selfprojection_kernel(tc, x, wo, wp, gain_o, bias_o, gain_p, bias_p, of
 
         ones = held.tile([PART, 1], F32, name="ones")
         nc.vector.memset(ones[:], 1.0)
-        identity = held.tile([2 * P_BLOCKS, 2 * P_BLOCKS], F32, name="identity")
-        make_identity(nc, identity[:])
+        shift_o_col = held.tile([PART, P_BLOCKS], F32, name="shift_o_col")
+        nc.gpsimd.tensor_scalar_add(shift_o_col[:], bias_o_col[:], 1.0)
 
         xs = held.tile([PART, C_BLOCKS, N], F32, name="xs")
         colsum_ps = psum.tile([N, 1], F32, name="colsum_ps")
-        rowsum = held.tile([PART, C_BLOCKS], F32, name="rowsum")
-        rowsum_bf = held.tile([PART, C_BLOCKS, PART], BF16, name="rowsum_bf")
+        rowsum_bf = held.tile([PART, C_BLOCKS], BF16, name="rowsum_bf")
         d_rep_ps = psum.tile([PART, P], F32, name="d_rep_ps")
         for b in range(C_BLOCKS):
             first, last = b == 0, b == C_BLOCKS - 1
             nc.scalar.activation(xs[:, b, :], x_blocks[b][:].indirect(offsets[:]), COPY)
             nc.tensor.matmul(colsum_ps[:], xs[:, b, :], ones[:], start=first, stop=last)
-            nc.vector.reduce_sum(rowsum[:, b : b + 1], xs[:, b, :], axis=mybir.AxisListType.X)
-            nc.vector.tensor_copy(rowsum_bf[:, b, :], rowsum[:, b : b + 1].to_broadcast([PART, PART]))
-            nc.tensor.matmul(d_rep_ps[:], rowsum_bf[:, b, :], wp_sb[:, b, :], start=first, stop=last)
+            with nc.allow_low_precision(reason="the sum is taken in float32 and rounded once to bfloat16"):
+                nc.vector.reduce_sum(rowsum_bf[:, b : b + 1], xs[:, b, :], axis=mybir.AxisListType.X)
+            nc.tensor.matmul(
+                d_rep_ps[:], rowsum_bf[:, b : b + 1].to_broadcast([PART, PART]), wp_sb[:, b, :], start=first, stop=last
+            )
 
-        colsum_bf = held.tile([N, PART], BF16, name="colsum_bf")
-        nc.scalar.copy(colsum_bf[:], colsum_ps[:].to_broadcast([N, PART]))
+        colsum_bf = held.tile([N, 1], BF16, name="colsum_bf")
+        nc.vector.tensor_copy(colsum_bf[:], colsum_ps[:])
         a_rep_ps = psum.tile([PART, P], F32, name="a_rep_ps")
-        nc.tensor.matmul(a_rep_ps[:], colsum_bf[:], wo_sb[:], start=True, stop=True)
+        nc.tensor.matmul(a_rep_ps[:], colsum_bf[:].to_broadcast([N, PART]), wo_sb[:], start=True, stop=True)
         a_col_ps = psum.tile([PART, P_BLOCKS], F32, name="a_col_ps")
         for b in range(P_BLOCKS):
             nc.tensor.matmul(
-                a_col_ps[:, b : b + 1], wo_sb[:, b * PART : (b + 1) * PART], colsum_bf[:, 0:1], start=True, stop=True
+                a_col_ps[:, b : b + 1], wo_sb[:, b * PART : (b + 1) * PART], colsum_bf[:], start=True, stop=True
             )
-
-        o_cols_ps = psum.tile([PART, 2 * P_BLOCKS], F32, name="o_cols_ps")
-        nc.tensor.matmul(o_cols_ps[:], o_rows[:], identity[:], start=True, stop=True)
-        gain_o_col = held.tile([PART, P_BLOCKS], F32, name="gain_o_col")
-        nc.vector.tensor_copy(gain_o_col[:], o_cols_ps[:, 0:P_BLOCKS])
-        shift_o_col = held.tile([PART, P_BLOCKS], F32, name="shift_o_col")
-        nc.vector.tensor_scalar_add(shift_o_col[:], o_cols_ps[:, P_BLOCKS : 2 * P_BLOCKS], 1.0)
 
         mean_var = held.tile([PART, 2, 2], F32, name="mean_var")
         for slot, row_ps in enumerate((d_rep_ps, a_rep_ps)):

@@ -24,13 +24,11 @@ FLOPS = 2 * C * N + 2 * N * P + 2 * C * P + P * P
 def tile_selfprojection_kernel(tc, x, wo, wp, gain_o, bias_o, gain_p, bias_p, offs, out):
     nc = tc.nc
     with tc.tile_pool(name="held", bufs=1) as held, tc.psum_pool(name="psum", bufs=1) as psum:
-        x_blocks = []
-        for b, queue in enumerate((nc.sync, nc.scalar)):
-            x_block = held.tile([PART, S], F32, name=f"x_block{b}")
-            queue.dma_start(x_block[:], x[b * PART : (b + 1) * PART, :])
-            x_blocks.append(x_block)
+        x_blocks = [held.tile([PART, S], F32, name=f"x_block{b}") for b in range(C_BLOCKS)]
         offsets = held.tile([PART, N // 16], U16, name="offsets")
+        nc.sync.dma_start(x_blocks[0][:], x[0:PART, :])
         nc.sync.dma_start(offsets[:], offs)
+        nc.sync.dma_start(x_blocks[1][:], x[PART : 2 * PART, :])
         wp_sb = held.tile([PART, C_BLOCKS, P], BF16, name="wp_sb")
         nc.sync.dma_start(wp_sb[:], wp.rearrange("(b c) q -> c b q", c=PART))
         wo_sb = held.tile([N, P], BF16, name="wo_sb")

@@ -7,8 +7,8 @@ ADD = mybir.AluOpType.add
 SUBTRACT = mybir.AluOpType.subtract
 MULT = mybir.AluOpType.mult
 COPY = mybir.ActivationFunctionType.Copy
-SQRT = mybir.ActivationFunctionType.Sqrt
 IDENTITY = mybir.ActivationFunctionType.Identity
+SQRT = mybir.ActivationFunctionType.Sqrt
 
 C, S, N, P = 256, 256, 128, 256
 PART = 128
@@ -33,14 +33,14 @@ def tile_selfprojection_kernel(tc, x, wo, wp, gain_o, bias_o, gain_p, bias_p, of
         nc.sync.dma_start(wp_sb[:], wp.rearrange("(b c) q -> c b q", c=PART))
         wo_sb = held.tile([N, P], BF16, name="wo_sb")
         nc.sync.dma_start(wo_sb[:], wo)
-        gain_o_col = held.tile([PART, P_BLOCKS], F32, name="gain_o_col")
-        nc.sync.dma_start(gain_o_col[:], gain_o.rearrange("(b p) one -> p (b one)", p=PART))
-        bias_o_col = held.tile([PART, P_BLOCKS], F32, name="bias_o_col")
-        nc.sync.dma_start(bias_o_col[:], bias_o.rearrange("(b p) one -> p (b one)", p=PART))
         gain_p_rep = held.tile([PART, P], F32, name="gain_p_rep")
         nc.sync.dma_start(gain_p_rep[:], gain_p.rearrange("q one -> (q one)").partition_broadcast(PART))
         bias_p_rep = held.tile([PART, P], F32, name="bias_p_rep")
         nc.sync.dma_start(bias_p_rep[:], bias_p.rearrange("q one -> (q one)").partition_broadcast(PART))
+        gain_o_col = held.tile([PART, P_BLOCKS], F32, name="gain_o_col")
+        nc.sync.dma_start(gain_o_col[:], gain_o.rearrange("(b p) one -> p (b one)", p=PART))
+        bias_o_col = held.tile([PART, P_BLOCKS], F32, name="bias_o_col")
+        nc.sync.dma_start(bias_o_col[:], bias_o.rearrange("(b p) one -> p (b one)", p=PART))
 
         zeros = held.tile([PART, PART], BF16, name="zeros")
         nc.vector.memset(zeros[:], 0.0)
@@ -81,31 +81,34 @@ def tile_selfprojection_kernel(tc, x, wo, wp, gain_o, bias_o, gain_p, bias_p, of
                 a_col_ps[:, b : b + 1], wo_sb[:, b * PART : (b + 1) * PART], colsum_bf[:], start=True, stop=True
             )
 
-        mean_var = held.tile([PART, 2, 2], F32, name="mean_var")
-        for slot, row_ps in enumerate((d_rep_ps, a_rep_ps)):
-            stats = held.tile([PART, BN_STATS_DIM], F32, name=f"stats{slot}")
-            nc.vector.bn_stats(stats[:], row_ps[:])
-            nc.vector.bn_aggr(mean_var[:, slot, :], stats[:])
-        inv_std = held.tile([PART, 2], F32, name="inv_std")
-        nc.scalar.activation(inv_std[:], mean_var[:, :, 1], SQRT, scale=P / (P - 1))
-        r_centred = held.tile([PART, P], F32, name="r_centred")
-        nc.vector.scalar_tensor_tensor(
-            r_centred[:], d_rep_ps[:], mean_var[:, 0, 0:1], gain_p_rep[:], op0=SUBTRACT, op1=MULT
-        )
-        o_centred = held.tile([PART, P_BLOCKS], F32, name="o_centred")
-        nc.vector.scalar_tensor_tensor(
-            o_centred[:], a_col_ps[:], mean_var[:, 1, 0:1], gain_o_col[:], op0=SUBTRACT, op1=MULT
-        )
-        nc.vector.tensor_scalar_add(inv_std[:], inv_std[:], EPS)
-        nc.vector.reciprocal(inv_std[:], inv_std[:])
+        def statistics(v, rep_ps):
+            stats = held.tile([PART, BN_STATS_DIM], F32, name=f"stats_{v}")
+            nc.vector.bn_stats(stats[:], rep_ps[:])
+            mean_var_eps = held.tile([PART, 3], F32, name=f"mean_var_eps_{v}")
+            nc.vector.memset(mean_var_eps[:, 2:3], EPS * EPS * (P - 1) / P)
+            nc.vector.bn_aggr(mean_var_eps[:, 0:2], stats[:])
+            roots = held.tile([PART, 2], F32, name=f"roots_{v}")
+            std_eps = held.tile([PART, 1], F32, name=f"std_eps_{v}")
+            nc.scalar.activation(roots[:], mean_var_eps[:, 1:3], SQRT, scale=P / (P - 1), accum_out=std_eps[:])
+            return mean_var_eps[:, 0:1], std_eps
 
-        o_col = held.tile([PART, P_BLOCKS], F32, name="o_col")
-        for b in range(P_BLOCKS):
-            nc.scalar.activation(
-                o_col[:, b : b + 1], o_centred[:, b : b + 1], IDENTITY, bias=shift_o_col[:, b : b + 1], scale=inv_std[:, 1:2]
-            )
+        mean_d, std_eps_d = statistics("d", d_rep_ps)
+        r_centred = held.tile([PART, P], F32, name="r_centred")
+        nc.vector.scalar_tensor_tensor(r_centred[:], d_rep_ps[:], mean_d, gain_p_rep[:], op0=SUBTRACT, op1=MULT)
+        mean_a, std_eps_a = statistics("a", a_rep_ps)
+        o_centred = held.tile([PART, P_BLOCKS], F32, name="o_centred")
+        nc.vector.scalar_tensor_tensor(o_centred[:], a_col_ps[:], mean_a, gain_o_col[:], op0=SUBTRACT, op1=MULT)
+
+        inv_std_d = held.tile([PART, 1], F32, name="inv_std_d")
+        nc.vector.reciprocal(inv_std_d[:], std_eps_d[:])
         r_less_1 = held.tile([PART, P], F32, name="r_less_1")
-        nc.vector.scalar_tensor_tensor(r_less_1[:], r_centred[:], inv_std[:, 0:1], bias_p_rep[:], op0=MULT, op1=ADD)
+        nc.vector.scalar_tensor_tensor(r_less_1[:], r_centred[:], inv_std_d[:], bias_p_rep[:], op0=MULT, op1=ADD)
+
+        inv_std_a = held.tile([PART, 1], F32, name="inv_std_a")
+        nc.vector.reciprocal(inv_std_a[:], std_eps_a[:])
+        o_col = held.tile([PART, P_BLOCKS], F32, name="o_col")
+        nc.vector.scalar_tensor_tensor(o_col[:], o_centred[:], inv_std_a[:], shift_o_col[:], op0=MULT, op1=ADD)
+
         out_block0 = held.tile([PART, P], F32, name="out_block0")
         nc.vector.tensor_scalar(out_block0[:], r_less_1[:], 1.0, o_col[:, 0:1], op0=ADD, op1=MULT)
         nc.sync.dma_start(out[0:PART, :], out_block0[:])

@@ -33,14 +33,14 @@ def tile_selfprojection_kernel(tc, x, wo, wp, gain_o, bias_o, gain_p, bias_p, of
         nc.sync.dma_start(wp_sb[:], wp.rearrange("(b c) q -> c b q", c=PART))
         wo_sb = held.tile([N, P], BF16, name="wo_sb")
         nc.sync.dma_start(wo_sb[:], wo)
-        gain_p_rep = held.tile([PART, P], F32, name="gain_p_rep")
-        nc.sync.dma_start(gain_p_rep[:], gain_p.rearrange("q one -> (q one)").partition_broadcast(PART))
-        bias_p_rep = held.tile([PART, P], F32, name="bias_p_rep")
-        nc.sync.dma_start(bias_p_rep[:], bias_p.rearrange("q one -> (q one)").partition_broadcast(PART))
         gain_o_col = held.tile([PART, P_BLOCKS], F32, name="gain_o_col")
         nc.sync.dma_start(gain_o_col[:], gain_o.rearrange("(b p) one -> p (b one)", p=PART))
         bias_o_col = held.tile([PART, P_BLOCKS], F32, name="bias_o_col")
         nc.sync.dma_start(bias_o_col[:], bias_o.rearrange("(b p) one -> p (b one)", p=PART))
+        gain_p_rep = held.tile([PART, P], F32, name="gain_p_rep")
+        nc.sync.dma_start(gain_p_rep[:], gain_p.rearrange("q one -> (q one)").partition_broadcast(PART))
+        bias_p_rep = held.tile([PART, P], F32, name="bias_p_rep")
+        nc.sync.dma_start(bias_p_rep[:], bias_p.rearrange("q one -> (q one)").partition_broadcast(PART))
 
         zeros = held.tile([PART, PART], BF16, name="zeros")
         nc.vector.memset(zeros[:], 0.0)

@@ -24,19 +24,21 @@ FLOPS = 2 * C * N + 2 * N * P + 2 * C * P + P * P
 def tile_selfprojection_kernel(tc, x, wo, wp, gain_o, bias_o, gain_p, bias_p, offs, out):
     nc = tc.nc
     with tc.tile_pool(name="held", bufs=1) as held, tc.psum_pool(name="psum", bufs=1) as psum:
+        x_split = x.rearrange("(c b) s -> c b s", b=C_BLOCKS)
+        out_split = out.rearrange("(p b) q -> p b q", b=P_BLOCKS)
         x_blocks = [held.tile([PART, S], F32, name=f"x_block{b}") for b in range(C_BLOCKS)]
         offsets = held.tile([PART, N // 16], U16, name="offsets")
-        nc.sync.dma_start(x_blocks[0][:], x[0:PART, :])
+        nc.sync.dma_start(x_blocks[0][:], x_split[:, 0, :])
         nc.sync.dma_start(offsets[:], offs)
-        nc.sync.dma_start(x_blocks[1][:], x[PART : 2 * PART, :])
+        nc.sync.dma_start(x_blocks[1][:], x_split[:, 1, :])
         wp_sb = held.tile([PART, C_BLOCKS, P], BF16, name="wp_sb")
-        nc.sync.dma_start(wp_sb[:], wp.rearrange("(b c) q -> c b q", c=PART))
+        nc.sync.dma_start(wp_sb[:], wp.rearrange("(c b) q -> c b q", b=C_BLOCKS))
         wo_sb = held.tile([N, P], BF16, name="wo_sb")
         nc.sync.dma_start(wo_sb[:], wo)
         gain_o_col = held.tile([PART, P_BLOCKS], F32, name="gain_o_col")
-        nc.sync.dma_start(gain_o_col[:], gain_o.rearrange("(b p) one -> p (b one)", p=PART))
+        nc.sync.dma_start(gain_o_col[:], gain_o.rearrange("(p b) one -> p (b one)", b=P_BLOCKS))
         bias_o_col = held.tile([PART, P_BLOCKS], F32, name="bias_o_col")
-        nc.sync.dma_start(bias_o_col[:], bias_o.rearrange("(b p) one -> p (b one)", p=PART))
+        nc.sync.dma_start(bias_o_col[:], bias_o.rearrange("(p b) one -> p (b one)", b=P_BLOCKS))
         gain_p_rep = held.tile([PART, P], F32, name="gain_p_rep")
         nc.sync.dma_start(gain_p_rep[:], gain_p.rearrange("q one -> (q one)").partition_broadcast(PART))
         bias_p_rep = held.tile([PART, P], F32, name="bias_p_rep")
@@ -76,10 +78,9 @@ def tile_selfprojection_kernel(tc, x, wo, wp, gain_o, bias_o, gain_p, bias_p, of
         a_rep_ps = psum.tile([PART, P], F32, name="a_rep_ps")
         nc.tensor.matmul(a_rep_ps[:], colsum_bf[:].to_broadcast([N, PART]), wo_sb[:], start=True, stop=True)
         a_col_ps = psum.tile([PART, P_BLOCKS], F32, name="a_col_ps")
+        wo_split = wo_sb[:].rearrange("j (p b) -> j b p", b=P_BLOCKS)
         for b in range(P_BLOCKS):
-            nc.tensor.matmul(
-                a_col_ps[:, b : b + 1], wo_sb[:, b * PART : (b + 1) * PART], colsum_bf[:], start=True, stop=True
-            )
+            nc.tensor.matmul(a_col_ps[:, b : b + 1], wo_split[:, b, :], colsum_bf[:], start=True, stop=True)
 
         def statistics(v, rep_ps):
             stats = held.tile([PART, BN_STATS_DIM], F32, name=f"stats_{v}")
@@ -111,7 +112,7 @@ def tile_selfprojection_kernel(tc, x, wo, wp, gain_o, bias_o, gain_p, bias_p, of
 
         out_block0 = held.tile([PART, P], F32, name="out_block0")
         nc.vector.tensor_scalar(out_block0[:], r_less_1[:], 1.0, o_col[:, 0:1], op0=ADD, op1=MULT)
-        nc.sync.dma_start(out[0:PART, :], out_block0[:])
+        nc.sync.dma_start(out_split[:, 0, :], out_block0[:])
         out_block1 = held.tile([PART, P], F32, name="out_block1")
         nc.scalar.activation(out_block1[:], r_less_1[:], IDENTITY, bias=o_col[:, 1:2], scale=o_col[:, 1:2])
-        nc.scalar.dma_start(out[PART : 2 * PART, :], out_block1[:])
+        nc.scalar.dma_start(out_split[:, 1, :], out_block1[:])

@@ -1,4 +1,5 @@
 import concourse.mybir as mybir
+from concourse.masks import make_identity
 
 F32 = mybir.dt.float32
 BF16 = mybir.dt.bfloat16
@@ -35,14 +36,10 @@ def tile_selfprojection_kernel(tc, x, wo, wp, gain_o, bias_o, gain_p, bias_p, of
         nc.sync.dma_start(wp_sb[:], wp.rearrange("(c b) q -> c b q", b=C_BLOCKS))
         wo_sb = held.tile([N, P], BF16, name="wo_sb")
         nc.sync.dma_start(wo_sb[:], wo)
-        gain_o_col = held.tile([PART, P_BLOCKS], F32, name="gain_o_col")
-        nc.sync.dma_start(gain_o_col[:], gain_o.rearrange("(p b) one -> p (b one)", b=P_BLOCKS))
-        bias_o_col = held.tile([PART, P_BLOCKS], F32, name="bias_o_col")
-        nc.sync.dma_start(bias_o_col[:], bias_o.rearrange("(p b) one -> p (b one)", b=P_BLOCKS))
-        gain_p_rep = held.tile([PART, P], F32, name="gain_p_rep")
-        nc.sync.dma_start(gain_p_rep[:], gain_p.rearrange("q one -> (q one)").partition_broadcast(PART))
-        bias_p_rep = held.tile([PART, P], F32, name="bias_p_rep")
-        nc.sync.dma_start(bias_p_rep[:], bias_p.rearrange("q one -> (q one)").partition_broadcast(PART))
+        small = {}
+        for name, vector in (("gain_p", gain_p), ("bias_p", bias_p), ("gain_o", gain_o), ("bias_o", bias_o)):
+            small[name] = held.tile([PART, P_BLOCKS], F32, name=f"{name}_col")
+            nc.sync.dma_start(small[name][:], vector.rearrange("(p b) one -> p (b one)", b=P_BLOCKS))
 
         zeros = held.tile([PART, PART], BF16, name="zeros")
         nc.vector.memset(zeros[:], 0.0)
@@ -56,8 +53,10 @@ def tile_selfprojection_kernel(tc, x, wo, wp, gain_o, bias_o, gain_p, bias_p, of
 
         ones = held.tile([PART, 1], F32, name="ones")
         nc.vector.memset(ones[:], 1.0)
+        identity = held.tile([PART, PART], F32, name="identity")
+        make_identity(nc, identity[:])
         shift_o_col = held.tile([PART, P_BLOCKS], F32, name="shift_o_col")
-        nc.gpsimd.tensor_scalar_add(shift_o_col[:], bias_o_col[:], 1.0)
+        nc.gpsimd.tensor_scalar_add(shift_o_col[:], small["bias_o"][:], 1.0)
 
         xs = held.tile([PART, C_BLOCKS, N], F32, name="xs")
         colsum_ps = psum.tile([N, 1], F32, name="colsum_ps")
@@ -72,6 +71,18 @@ def tile_selfprojection_kernel(tc, x, wo, wp, gain_o, bias_o, gain_p, bias_p, of
             nc.tensor.matmul(
                 d_rep_ps[:], rowsum_bf[:, b : b + 1].to_broadcast([PART, PART]), wp_sb[:, b, :], start=first, stop=last
             )
+
+        d_col_ps = psum.tile([PART, P_BLOCKS], F32, name="d_col_ps")
+        wp_split = wp_sb[:].rearrange("c b (p e) -> c b e p", e=P_BLOCKS)
+        for e in range(P_BLOCKS):
+            for b in range(C_BLOCKS):
+                nc.tensor.matmul(
+                    d_col_ps[:, e : e + 1],
+                    wp_split[:, b, e, :],
+                    rowsum_bf[:, b : b + 1],
+                    start=b == 0,
+                    stop=b == C_BLOCKS - 1,
+                )
 
         colsum_bf = held.tile([N, 1], BF16, name="colsum_bf")
         nc.vector.tensor_copy(colsum_bf[:], colsum_ps[:])
@@ -94,25 +105,32 @@ def tile_selfprojection_kernel(tc, x, wo, wp, gain_o, bias_o, gain_p, bias_p, of
             return mean_var_eps[:, 0:1], std_eps
 
         mean_d, std_eps_d = statistics("d", d_rep_ps)
-        r_centred = held.tile([PART, P], F32, name="r_centred")
-        nc.vector.scalar_tensor_tensor(r_centred[:], d_rep_ps[:], mean_d, gain_p_rep[:], op0=SUBTRACT, op1=MULT)
-        mean_a, std_eps_a = statistics("a", a_rep_ps)
-        o_centred = held.tile([PART, P_BLOCKS], F32, name="o_centred")
-        nc.vector.scalar_tensor_tensor(o_centred[:], a_col_ps[:], mean_a, gain_o_col[:], op0=SUBTRACT, op1=MULT)
-
+        r_centred = held.tile([PART, P_BLOCKS], F32, name="r_centred")
+        nc.vector.scalar_tensor_tensor(r_centred[:], d_col_ps[:], mean_d, small["gain_p"][:], op0=SUBTRACT, op1=MULT)
         inv_std_d = held.tile([PART, 1], F32, name="inv_std_d")
         nc.vector.reciprocal(inv_std_d[:], std_eps_d[:])
-        r_less_1 = held.tile([PART, P], F32, name="r_less_1")
-        nc.vector.scalar_tensor_tensor(r_less_1[:], r_centred[:], inv_std_d[:], bias_p_rep[:], op0=MULT, op1=ADD)
+        r_less_1 = held.tile([PART, P_BLOCKS], F32, name="r_less_1")
+        nc.vector.scalar_tensor_tensor(
+            r_less_1[:], r_centred[:], inv_std_d[:], small["bias_p"][:], op0=MULT, op1=ADD
+        )
+        r_rows = {}
+        for engine in ("vector", "scalar"):
+            r_ps = psum.tile([PART, P_BLOCKS, PART], F32, name=f"r_ps_{engine}")
+            for e in range(P_BLOCKS):
+                nc.tensor.transpose(r_ps[:, e, :], r_less_1[:, e : e + 1].to_broadcast([PART, PART]), identity[:])
+            r_rows[engine] = r_ps[:].rearrange("m e p -> m p e")
 
+        mean_a, std_eps_a = statistics("a", a_rep_ps)
+        o_centred = held.tile([PART, P_BLOCKS], F32, name="o_centred")
+        nc.vector.scalar_tensor_tensor(o_centred[:], a_col_ps[:], mean_a, small["gain_o"][:], op0=SUBTRACT, op1=MULT)
         inv_std_a = held.tile([PART, 1], F32, name="inv_std_a")
         nc.vector.reciprocal(inv_std_a[:], std_eps_a[:])
         o_col = held.tile([PART, P_BLOCKS], F32, name="o_col")
         nc.vector.scalar_tensor_tensor(o_col[:], o_centred[:], inv_std_a[:], shift_o_col[:], op0=MULT, op1=ADD)
 
-        out_block0 = held.tile([PART, P], F32, name="out_block0")
-        nc.vector.tensor_scalar(out_block0[:], r_less_1[:], 1.0, o_col[:, 0:1], op0=ADD, op1=MULT)
-        nc.sync.dma_start(out_split[:, 0, :], out_block0[:])
-        out_block1 = held.tile([PART, P], F32, name="out_block1")
-        nc.scalar.activation(out_block1[:], r_less_1[:], IDENTITY, bias=o_col[:, 1:2], scale=o_col[:, 1:2])
-        nc.scalar.dma_start(out_split[:, 1, :], out_block1[:])
+        out_block0 = held.tile([PART, PART, P_BLOCKS], F32, name="out_block0")
+        nc.vector.tensor_scalar(out_block0[:], r_rows["vector"], 1.0, o_col[:, 0:1], op0=ADD, op1=MULT)
+        nc.sync.dma_start(out_split[:, 0, :], out_block0[:].rearrange("m p e -> m (p e)"))
+        out_block1 = held.tile([PART, PART, P_BLOCKS], F32, name="out_block1")
+        nc.scalar.activation(out_block1[:], r_rows["scalar"], IDENTITY, bias=o_col[:, 1:2], scale=o_col[:, 1:2])
+        nc.scalar.dma_start(out_split[:, 1, :], out_block1[:].rearrange("m p e -> m (p e)"))

@@ -26,7 +26,6 @@ def tile_selfprojection_kernel(tc, x, wo, wp, gain_o, bias_o, gain_p, bias_p, of
     nc = tc.nc
     with tc.tile_pool(name="held", bufs=1) as held, tc.psum_pool(name="psum", bufs=1) as psum:
         x_split = x.rearrange("(c b) s -> c b s", b=C_BLOCKS)
-        out_split = out.rearrange("(p b) q -> p b q", b=P_BLOCKS)
         x_blocks = [held.tile([PART, S], F32, name=f"x_block{b}") for b in range(C_BLOCKS)]
         offsets = held.tile([PART, N // 16], U16, name="offsets")
         nc.sync.dma_start(x_blocks[0][:], x_split[:, 0, :])
@@ -37,9 +36,14 @@ def tile_selfprojection_kernel(tc, x, wo, wp, gain_o, bias_o, gain_p, bias_p, of
         wo_sb = held.tile([N, P], BF16, name="wo_sb")
         nc.sync.dma_start(wo_sb[:], wo)
         small = {}
-        for name, vector in (("gain_p", gain_p), ("bias_p", bias_p), ("gain_o", gain_o), ("bias_o", bias_o)):
+        for name, vector, cut in (
+            ("gain_p", gain_p, "(e m) one -> m (e one)"),
+            ("bias_p", bias_p, "(e m) one -> m (e one)"),
+            ("gain_o", gain_o, "(m e) one -> m (e one)"),
+            ("bias_o", bias_o, "(m e) one -> m (e one)"),
+        ):
             small[name] = held.tile([PART, P_BLOCKS], F32, name=f"{name}_col")
-            nc.sync.dma_start(small[name][:], vector.rearrange("(p b) one -> p (b one)", b=P_BLOCKS))
+            nc.sync.dma_start(small[name][:], vector.rearrange(cut, e=P_BLOCKS))
 
         zeros = held.tile([PART, PART], BF16, name="zeros")
         nc.vector.memset(zeros[:], 0.0)
@@ -73,12 +77,11 @@ def tile_selfprojection_kernel(tc, x, wo, wp, gain_o, bias_o, gain_p, bias_p, of
             )
 
         d_col_ps = psum.tile([PART, P_BLOCKS], F32, name="d_col_ps")
-        wp_split = wp_sb[:].rearrange("c b (p e) -> c b e p", e=P_BLOCKS)
         for e in range(P_BLOCKS):
             for b in range(C_BLOCKS):
                 nc.tensor.matmul(
                     d_col_ps[:, e : e + 1],
-                    wp_split[:, b, e, :],
+                    wp_sb[:, b, e * PART : (e + 1) * PART],
                     rowsum_bf[:, b : b + 1],
                     start=b == 0,
                     stop=b == C_BLOCKS - 1,
@@ -113,12 +116,11 @@ def tile_selfprojection_kernel(tc, x, wo, wp, gain_o, bias_o, gain_p, bias_p, of
         nc.vector.scalar_tensor_tensor(
             r_less_1[:], r_centred[:], inv_std_d[:], small["bias_p"][:], op0=MULT, op1=ADD
         )
-        r_rows = {}
-        for engine in ("vector", "scalar"):
-            r_ps = psum.tile([PART, P_BLOCKS, PART], F32, name=f"r_ps_{engine}")
-            for e in range(P_BLOCKS):
-                nc.tensor.transpose(r_ps[:, e, :], r_less_1[:, e : e + 1].to_broadcast([PART, PART]), identity[:])
-            r_rows[engine] = r_ps[:].rearrange("m e p -> m p e")
+        r_halves = []
+        for e in range(P_BLOCKS):
+            r_half_ps = psum.tile([PART, PART], F32, name=f"r_half_ps{e}")
+            nc.tensor.transpose(r_half_ps[:], r_less_1[:, e : e + 1].to_broadcast([PART, PART]), identity[:])
+            r_halves.append(r_half_ps)
 
         mean_a, std_eps_a = statistics("a", a_rep_ps)
         o_centred = held.tile([PART, P_BLOCKS], F32, name="o_centred")
@@ -128,9 +130,17 @@ def tile_selfprojection_kernel(tc, x, wo, wp, gain_o, bias_o, gain_p, bias_p, of
         o_col = held.tile([PART, P_BLOCKS], F32, name="o_col")
         nc.vector.scalar_tensor_tensor(o_col[:], o_centred[:], inv_std_a[:], shift_o_col[:], op0=MULT, op1=ADD)
 
-        out_block0 = held.tile([PART, PART, P_BLOCKS], F32, name="out_block0")
-        nc.vector.tensor_scalar(out_block0[:], r_rows["vector"], 1.0, o_col[:, 0:1], op0=ADD, op1=MULT)
-        nc.sync.dma_start(out_split[:, 0, :], out_block0[:].rearrange("m p e -> m (p e)"))
-        out_block1 = held.tile([PART, PART, P_BLOCKS], F32, name="out_block1")
-        nc.scalar.activation(out_block1[:], r_rows["scalar"], IDENTITY, bias=o_col[:, 1:2], scale=o_col[:, 1:2])
-        nc.scalar.dma_start(out_split[:, 1, :], out_block1[:].rearrange("m p e -> m (p e)"))
+        out_sb = held.tile([PART, P_BLOCKS, P], F32, name="out_sb")
+        shape = [PART, P_BLOCKS, PART]
+        nc.vector.scalar_tensor_tensor(
+            out_sb[:, :, 0:PART],
+            r_halves[0][:].unsqueeze(1).to_broadcast(shape),
+            1.0,
+            o_col[:].unsqueeze(2).to_broadcast(shape),
+            op0=ADD,
+            op1=MULT,
+        )
+        for b in range(P_BLOCKS):
+            o_b = o_col[:, b : b + 1]
+            nc.scalar.activation(out_sb[:, b, PART:P], r_halves[1][:], IDENTITY, bias=o_b, scale=o_b)
+        nc.sync.dma_start(out.rearrange("(p b) q -> p (b q)", b=P_BLOCKS), out_sb[:].rearrange("p b q -> p (b q)"))

import concourse.mybir as mybir
from concourse.masks import make_identity

F32 = mybir.dt.float32
BF16 = mybir.dt.bfloat16
U16 = mybir.dt.uint16
ADD = mybir.AluOpType.add
SUBTRACT = mybir.AluOpType.subtract
MULT = mybir.AluOpType.mult
COPY = mybir.ActivationFunctionType.Copy
IDENTITY = mybir.ActivationFunctionType.Identity
SQRT = mybir.ActivationFunctionType.Sqrt

C, S, N, P = 256, 256, 128, 256
PART = 128
C_BLOCKS = C // PART
P_BLOCKS = P // PART
EPS = 1e-05
WARM_UP_MATMULS = 20
BN_STATS_DIM = 6

FLOPS = 2 * C * N + 2 * N * P + 2 * C * P + P * P


def tile_selfprojection_kernel(tc, x, wo, wp, gain_o, bias_o, gain_p, bias_p, offs, out):
    nc = tc.nc
    with tc.tile_pool(name="held", bufs=1) as held, tc.psum_pool(name="psum", bufs=1) as psum:
        x_split = x.rearrange("(c b) s -> c b s", b=C_BLOCKS)
        x_blocks = [held.tile([PART, S], F32, name=f"x_block{b}") for b in range(C_BLOCKS)]
        offsets = held.tile([PART, N // 16], U16, name="offsets")
        nc.sync.dma_start(x_blocks[0][:], x_split[:, 0, :])
        nc.sync.dma_start(offsets[:], offs)
        nc.sync.dma_start(x_blocks[1][:], x_split[:, 1, :])
        wp_sb = held.tile([PART, C_BLOCKS, P], BF16, name="wp_sb")
        nc.sync.dma_start(wp_sb[:], wp.rearrange("(c b) q -> c b q", b=C_BLOCKS))
        wo_sb = held.tile([N, P], BF16, name="wo_sb")
        nc.sync.dma_start(wo_sb[:], wo)
        small = {}
        for name, vector, cut in (
            ("gain_p", gain_p, "(e m) one -> m (e one)"),
            ("bias_p", bias_p, "(e m) one -> m (e one)"),
            ("gain_o", gain_o, "(m e) one -> m (e one)"),
            ("bias_o", bias_o, "(m e) one -> m (e one)"),
        ):
            small[name] = held.tile([PART, P_BLOCKS], F32, name=f"{name}_col")
            nc.sync.dma_start(small[name][:], vector.rearrange(cut, e=P_BLOCKS))

        zeros = held.tile([PART, PART], BF16, name="zeros")
        nc.vector.memset(zeros[:], 0.0)
        unread_ps = psum.tile([PART, PART], F32, name="unread_ps")
        for w in range(WARM_UP_MATMULS):
            nc.tensor.matmul(unread_ps[:], zeros[:], zeros[:], start=True, stop=True)

        scratch = held.tile([PART, 1], F32, name="scratch")
        nc.vector.memset(scratch[:], 1.0)
        nc.scalar.activation(scratch[:], scratch[:], SQRT)

        ones = held.tile([PART, 1], F32, name="ones")
        nc.vector.memset(ones[:], 1.0)
        identity = held.tile([PART, PART], F32, name="identity")
        make_identity(nc, identity[:])
        shift_o_col = held.tile([PART, P_BLOCKS], F32, name="shift_o_col")
        nc.gpsimd.tensor_scalar_add(shift_o_col[:], small["bias_o"][:], 1.0)

        xs = held.tile([PART, C_BLOCKS, N], F32, name="xs")
        colsum_ps = psum.tile([N, 1], F32, name="colsum_ps")
        rowsum_bf = held.tile([PART, C_BLOCKS], BF16, name="rowsum_bf")
        d_rep_ps = psum.tile([PART, P], F32, name="d_rep_ps")
        for b in range(C_BLOCKS):
            first, last = b == 0, b == C_BLOCKS - 1
            nc.scalar.activation(xs[:, b, :], x_blocks[b][:].indirect(offsets[:]), COPY)
            nc.tensor.matmul(colsum_ps[:], xs[:, b, :], ones[:], start=first, stop=last)
            with nc.allow_low_precision(reason="the sum is taken in float32 and rounded once to bfloat16"):
                nc.vector.reduce_sum(rowsum_bf[:, b : b + 1], xs[:, b, :], axis=mybir.AxisListType.X)
            nc.tensor.matmul(
                d_rep_ps[:], rowsum_bf[:, b : b + 1].to_broadcast([PART, PART]), wp_sb[:, b, :], start=first, stop=last
            )

        d_col_ps = psum.tile([PART, P_BLOCKS], F32, name="d_col_ps")
        for e in range(P_BLOCKS):
            for b in range(C_BLOCKS):
                nc.tensor.matmul(
                    d_col_ps[:, e : e + 1],
                    wp_sb[:, b, e * PART : (e + 1) * PART],
                    rowsum_bf[:, b : b + 1],
                    start=b == 0,
                    stop=b == C_BLOCKS - 1,
                )

        colsum_bf = held.tile([N, 1], BF16, name="colsum_bf")
        nc.vector.tensor_copy(colsum_bf[:], colsum_ps[:])
        a_rep_ps = psum.tile([PART, P], F32, name="a_rep_ps")
        nc.tensor.matmul(a_rep_ps[:], colsum_bf[:].to_broadcast([N, PART]), wo_sb[:], start=True, stop=True)
        a_col_ps = psum.tile([PART, P_BLOCKS], F32, name="a_col_ps")
        wo_split = wo_sb[:].rearrange("j (p b) -> j b p", b=P_BLOCKS)
        for b in range(P_BLOCKS):
            nc.tensor.matmul(a_col_ps[:, b : b + 1], wo_split[:, b, :], colsum_bf[:], start=True, stop=True)

        def statistics(v, rep_ps):
            stats = held.tile([PART, BN_STATS_DIM], F32, name=f"stats_{v}")
            nc.vector.bn_stats(stats[:], rep_ps[:])
            mean_var_eps = held.tile([PART, 3], F32, name=f"mean_var_eps_{v}")
            nc.vector.memset(mean_var_eps[:, 2:3], EPS * EPS * (P - 1) / P)
            nc.vector.bn_aggr(mean_var_eps[:, 0:2], stats[:])
            roots = held.tile([PART, 2], F32, name=f"roots_{v}")
            std_eps = held.tile([PART, 1], F32, name=f"std_eps_{v}")
            nc.scalar.activation(roots[:], mean_var_eps[:, 1:3], SQRT, scale=P / (P - 1), accum_out=std_eps[:])
            return mean_var_eps[:, 0:1], std_eps

        mean_d, std_eps_d = statistics("d", d_rep_ps)
        r_centred = held.tile([PART, P_BLOCKS], F32, name="r_centred")
        nc.vector.scalar_tensor_tensor(r_centred[:], d_col_ps[:], mean_d, small["gain_p"][:], op0=SUBTRACT, op1=MULT)
        inv_std_d = held.tile([PART, 1], F32, name="inv_std_d")
        nc.vector.reciprocal(inv_std_d[:], std_eps_d[:])
        r_less_1 = held.tile([PART, P_BLOCKS], F32, name="r_less_1")
        nc.vector.scalar_tensor_tensor(
            r_less_1[:], r_centred[:], inv_std_d[:], small["bias_p"][:], op0=MULT, op1=ADD
        )
        r_halves = []
        for e in range(P_BLOCKS):
            r_half_ps = psum.tile([PART, PART], F32, name=f"r_half_ps{e}")
            nc.tensor.transpose(r_half_ps[:], r_less_1[:, e : e + 1].to_broadcast([PART, PART]), identity[:])
            r_halves.append(r_half_ps)

        mean_a, std_eps_a = statistics("a", a_rep_ps)
        o_centred = held.tile([PART, P_BLOCKS], F32, name="o_centred")
        nc.vector.scalar_tensor_tensor(o_centred[:], a_col_ps[:], mean_a, small["gain_o"][:], op0=SUBTRACT, op1=MULT)
        inv_std_a = held.tile([PART, 1], F32, name="inv_std_a")
        nc.vector.reciprocal(inv_std_a[:], std_eps_a[:])
        o_col = held.tile([PART, P_BLOCKS], F32, name="o_col")
        nc.vector.scalar_tensor_tensor(o_col[:], o_centred[:], inv_std_a[:], shift_o_col[:], op0=MULT, op1=ADD)

        out_sb = held.tile([PART, P_BLOCKS, P], F32, name="out_sb")
        shape = [PART, P_BLOCKS, PART]
        nc.vector.scalar_tensor_tensor(
            out_sb[:, :, 0:PART],
            r_halves[0][:].unsqueeze(1).to_broadcast(shape),
            1.0,
            o_col[:].unsqueeze(2).to_broadcast(shape),
            op0=ADD,
            op1=MULT,
        )
        for b in range(P_BLOCKS):
            o_b = o_col[:, b : b + 1]
            nc.scalar.activation(out_sb[:, b, PART:P], r_halves[1][:], IDENTITY, bias=o_b, scale=o_b)
        nc.sync.dma_start(out.rearrange("(p b) q -> p (b q)", b=P_BLOCKS), out_sb[:].rearrange("p b q -> p (b q)"))
